import numpy as np
import ml_dtypes

BF16 = ml_dtypes.bfloat16


def bf(x):
    return np.asarray(x, np.float32).astype(BF16)


def f32(x):
    return np.asarray(x, np.float32)


def f64(x):
    return np.asarray(x).astype(np.float64)


def striped(idx):
    return np.tile(idx.reshape(-1, 16).T, (8, 1))


F, H, M, S, E, N = 128, 4, 512, 2048, 512, 1024


def setup_inputs():
    return {"x": bf(np.random.standard_normal((F, S))), "wq": bf(np.random.standard_normal((F, M)) / np.sqrt(F)), "bq": f32(0.1 * np.random.standard_normal((M, 1))), "wk": bf(np.random.standard_normal((F, M)) / np.sqrt(F)), "bk": f32(0.1 * np.random.standard_normal((M, 1))), "offs": striped(np.random.permutation(np.tile(np.arange(S), 2))[:N])}


def reference(x, wq, bq, wk, bk, offs):
    idx = offs[:16].T.reshape(-1)
    t = f64(x)
    query = f64(wq).T @ t[:, idx[:E]] + f64(bq)
    key = f64(wk).T @ t[:, idx[E:]] + f64(bk)
    return query * key

@@ -1,0 +1,56 @@
+import concourse.mybir as mybir
+
+BF16, F32, U16 = mybir.dt.bfloat16, mybir.dt.float32, mybir.dt.uint16
+ADD, MULT = mybir.AluOpType.add, mybir.AluOpType.mult
+IDENTITY = mybir.ActivationFunctionType.Identity
+
+P = 128
+NODES = 2048
+HEADS = 4
+EDGES = 512
+LIST = 2 * EDGES
+PER_COLUMN = 16
+
+FLOPS = 2 * P * (HEADS * P) * LIST
+
+
+def tile_attentionheads_kernel(tc, x, wq, bq, wk, bk, offs, out):
+    nc = tc.nc
+    with (
+        tc.tile_pool(name="held", bufs=1) as held,
+        tc.tile_pool(name="work", bufs=HEADS) as work,
+        tc.psum_pool(name="psum", bufs=HEADS) as psum,
+    ):
+        offsets = held.tile([P, LIST // PER_COLUMN], U16, name="offsets")
+        nc.sync.dma_start(offsets[:], offs)
+        nodes = held.tile([P, NODES], BF16, name="nodes")
+        nc.sync.dma_start(nodes[:], x)
+        wq_sb = held.tile([P, HEADS * P], BF16, name="wq_sb")
+        nc.scalar.dma_start(wq_sb[:], wq)
+        wk_sb = held.tile([P, HEADS * P], BF16, name="wk_sb")
+        nc.scalar.dma_start(wk_sb[:], wk)
+
+        bq_sb = held.tile([P, HEADS], F32, name="bq_sb")
+        bk_sb = held.tile([P, HEADS], F32, name="bk_sb")
+        with nc.allow_non_contiguous_dma(reason="512 single float32 biases, one to a partition"):
+            nc.scalar.dma_start(bq_sb[:], bq.rearrange("(h r) o -> r (h o)", r=P))
+            nc.scalar.dma_start(bk_sb[:], bk.rearrange("(h r) o -> r (h o)", r=P))
+
+        half = EDGES // PER_COLUMN
+        query_nodes = nodes[:].indirect(offsets[:, 0:half])
+        key_nodes = nodes[:].indirect(offsets[:, half : 2 * half])
+
+        for h in range(HEADS):
+            rows = slice(h * P, (h + 1) * P)
+            query_ps = psum.tile([P, EDGES], F32, name="query_ps")
+            nc.tensor.matmul(query_ps[:], wq_sb[:, rows], query_nodes, start=True, stop=True)
+            key_ps = psum.tile([P, EDGES], F32, name="key_ps")
+            nc.tensor.matmul(key_ps[:], wk_sb[:, rows], key_nodes, start=True, stop=True)
+
+            query_sb = work.tile([P, EDGES], F32, name="query_sb")
+            nc.scalar.activation(query_sb[:], query_ps[:], IDENTITY, bias=bq_sb[:, h : h + 1])
+            product = work.tile([P, EDGES], F32, name="product")
+            nc.vector.scalar_tensor_tensor(
+                product[:], key_ps[:], bk_sb[:, h : h + 1], query_sb[:], ADD, MULT
+            )
+            nc.sync.dma_start(out[rows, :], product[:])

@@ -11,6 +11,8 @@ EDGES = 512
 LIST = 2 * EDGES
 PER_COLUMN = 16
 
+WARM_MATMULS = 6
+
 FLOPS = 2 * P * (HEADS * P) * LIST
 
 
@@ -19,7 +21,8 @@ def tile_attentionheads_kernel(tc, x, wq, bq, wk, bk, offs, out):
     with (
         tc.tile_pool(name="held", bufs=1) as held,
         tc.tile_pool(name="work", bufs=HEADS) as work,
-        tc.psum_pool(name="psum", bufs=HEADS) as psum,
+        tc.psum_pool(name="psum", bufs=3) as psum,
+        tc.psum_pool(name="spare", bufs=1) as spare,
     ):
         offsets = held.tile([P, LIST // PER_COLUMN], U16, name="offsets")
         nc.sync.dma_start(offsets[:], offs)
@@ -35,6 +38,12 @@ def tile_attentionheads_kernel(tc, x, wq, bq, wk, bk, offs, out):
         with nc.allow_non_contiguous_dma(reason="512 single float32 biases, one to a partition"):
             nc.scalar.dma_start(bq_sb[:], bq.rearrange("(h r) o -> r (h o)", r=P))
             nc.scalar.dma_start(bk_sb[:], bk.rearrange("(h r) o -> r (h o)", r=P))
+
+        zeros = held.tile([P, EDGES], BF16, name="zeros")
+        nc.vector.memset(zeros[:], 0.0)
+        unread = spare.tile([P, EDGES], F32, name="unread")
+        for i in range(WARM_MATMULS):
+            nc.tensor.matmul(unread[:], zeros[:, 0:P], zeros[:], start=True, stop=True)
 
         half = EDGES // PER_COLUMN
         query_nodes = nodes[:].indirect(offsets[:, 0:half])

@@ -10,8 +10,7 @@ HEADS = 4
 EDGES = 512
 LIST = 2 * EDGES
 PER_COLUMN = 16
-
-WARM_MATMULS = 6
+BLOCK = 32
 
 FLOPS = 2 * P * (HEADS * P) * LIST
 
@@ -21,8 +20,7 @@ def tile_attentionheads_kernel(tc, x, wq, bq, wk, bk, offs, out):
     with (
         tc.tile_pool(name="held", bufs=1) as held,
         tc.tile_pool(name="work", bufs=HEADS) as work,
-        tc.psum_pool(name="psum", bufs=3) as psum,
-        tc.psum_pool(name="spare", bufs=1) as spare,
+        tc.psum_pool(name="psum", bufs=HEADS) as psum,
     ):
         offsets = held.tile([P, LIST // PER_COLUMN], U16, name="offsets")
         nc.sync.dma_start(offsets[:], offs)
@@ -33,17 +31,16 @@ def tile_attentionheads_kernel(tc, x, wq, bq, wk, bk, offs, out):
         wk_sb = held.tile([P, HEADS * P], BF16, name="wk_sb")
         nc.scalar.dma_start(wk_sb[:], wk)
 
-        bq_sb = held.tile([P, HEADS], F32, name="bq_sb")
-        bk_sb = held.tile([P, HEADS], F32, name="bk_sb")
-        with nc.allow_non_contiguous_dma(reason="512 single float32 biases, one to a partition"):
-            nc.scalar.dma_start(bq_sb[:], bq.rearrange("(h r) o -> r (h o)", r=P))
-            nc.scalar.dma_start(bk_sb[:], bk.rearrange("(h r) o -> r (h o)", r=P))
-
-        zeros = held.tile([P, EDGES], BF16, name="zeros")
-        nc.vector.memset(zeros[:], 0.0)
-        unread = spare.tile([P, EDGES], F32, name="unread")
-        for i in range(WARM_MATMULS):
-            nc.tensor.matmul(unread[:], zeros[:, 0:P], zeros[:], start=True, stop=True)
+        packed = held.tile([P, BLOCK], F32, name="packed", align_bytes=64)
+        nc.vector.memset(packed[:], 0.0)
+        bq_runs = bq.rearrange("(h b i) o -> h b (i o)", h=HEADS, i=BLOCK)
+        bk_runs = bk.rearrange("(h b i) o -> h b (i o)", h=HEADS, i=BLOCK)
+        for b in range(P // BLOCK):
+            first = b * BLOCK
+            nc.sync.dma_start(packed[first : first + HEADS, :], bq_runs[:, b, :])
+            nc.gpsimd.dma_start(packed[first + HEADS : first + 2 * HEADS, :], bk_runs[:, b, :])
+        biases = held.tile([P, BLOCK], F32, name="biases", align_bytes=64)
+        nc.vector.transpose(biases[:], packed[:])
 
         half = EDGES // PER_COLUMN
         query_nodes = nodes[:].indirect(offsets[:, 0:half])
@@ -57,9 +54,9 @@ def tile_attentionheads_kernel(tc, x, wq, bq, wk, bk, offs, out):
             nc.tensor.matmul(key_ps[:], wk_sb[:, rows], key_nodes, start=True, stop=True)
 
             query_sb = work.tile([P, EDGES], F32, name="query_sb")
-            nc.scalar.activation(query_sb[:], query_ps[:], IDENTITY, bias=bq_sb[:, h : h + 1])
+            nc.scalar.activation(query_sb[:], query_ps[:], IDENTITY, bias=biases[:, h : h + 1])
             product = work.tile([P, EDGES], F32, name="product")
             nc.vector.scalar_tensor_tensor(
-                product[:], key_ps[:], bk_sb[:, h : h + 1], query_sb[:], ADD, MULT
+                product[:], key_ps[:], biases[:, HEADS + h : HEADS + h + 1], query_sb[:], ADD, MULT
             )
             nc.sync.dma_start(out[rows, :], product[:])

@@ -6,57 +6,54 @@ IDENTITY = mybir.ActivationFunctionType.Identity
 
 P = 128
 NODES = 2048
-HEADS = 4
+BLOCKS = 4
 EDGES = 512
 LIST = 2 * EDGES
 PER_COLUMN = 16
-BLOCK = 32
 
-FLOPS = 2 * P * (HEADS * P) * LIST
+FLOPS = 2 * P * (BLOCKS * P) * LIST
 
 
 def tile_attentionheads_kernel(tc, x, wq, bq, wk, bk, offs, out):
     nc = tc.nc
     with (
         tc.tile_pool(name="held", bufs=1) as held,
-        tc.tile_pool(name="work", bufs=HEADS) as work,
-        tc.psum_pool(name="psum", bufs=HEADS) as psum,
+        tc.tile_pool(name="work", bufs=BLOCKS) as work,
+        tc.psum_pool(name="psum", bufs=BLOCKS) as psum,
     ):
         offsets = held.tile([P, LIST // PER_COLUMN], U16, name="offsets")
         nc.sync.dma_start(offsets[:], offs)
         nodes = held.tile([P, NODES], BF16, name="nodes")
         nc.sync.dma_start(nodes[:], x)
-        wq_sb = held.tile([P, HEADS * P], BF16, name="wq_sb")
+        wq_sb = held.tile([P, BLOCKS * P], BF16, name="wq_sb")
         nc.scalar.dma_start(wq_sb[:], wq)
-        wk_sb = held.tile([P, HEADS * P], BF16, name="wk_sb")
+        wk_sb = held.tile([P, BLOCKS * P], BF16, name="wk_sb")
         nc.scalar.dma_start(wk_sb[:], wk)
 
-        packed = held.tile([P, BLOCK], F32, name="packed", align_bytes=64)
-        nc.vector.memset(packed[:], 0.0)
-        bq_runs = bq.rearrange("(h b i) o -> h b (i o)", h=HEADS, i=BLOCK)
-        bk_runs = bk.rearrange("(h b i) o -> h b (i o)", h=HEADS, i=BLOCK)
-        for b in range(P // BLOCK):
-            first = b * BLOCK
-            nc.sync.dma_start(packed[first : first + HEADS, :], bq_runs[:, b, :])
-            nc.gpsimd.dma_start(packed[first + HEADS : first + 2 * HEADS, :], bk_runs[:, b, :])
-        biases = held.tile([P, BLOCK], F32, name="biases", align_bytes=64)
-        nc.vector.transpose(biases[:], packed[:])
+        bq_sb = held.tile([P, BLOCKS], F32, name="bq_sb")
+        nc.scalar.dma_start(bq_sb[:], bq.rearrange("(r b) o -> r (b o)", b=BLOCKS))
+        bk_sb = held.tile([P, BLOCKS], F32, name="bk_sb")
+        nc.scalar.dma_start(bk_sb[:], bk.rearrange("(r b) o -> r (b o)", b=BLOCKS))
+        wq_blocks = held.tile([P, BLOCKS, P], BF16, name="wq_blocks")
+        nc.vector.tensor_copy(wq_blocks[:], wq_sb[:].rearrange("f (r b) -> f b r", b=BLOCKS))
+        wk_blocks = held.tile([P, BLOCKS, P], BF16, name="wk_blocks")
+        nc.scalar.activation(wk_blocks[:], wk_sb[:].rearrange("f (r b) -> f b r", b=BLOCKS), IDENTITY)
+        out_blocks = out.rearrange("(r b) e -> b r e", b=BLOCKS)
 
         half = EDGES // PER_COLUMN
         query_nodes = nodes[:].indirect(offsets[:, 0:half])
         key_nodes = nodes[:].indirect(offsets[:, half : 2 * half])
 
-        for h in range(HEADS):
-            rows = slice(h * P, (h + 1) * P)
+        for b in range(BLOCKS):
             query_ps = psum.tile([P, EDGES], F32, name="query_ps")
-            nc.tensor.matmul(query_ps[:], wq_sb[:, rows], query_nodes, start=True, stop=True)
+            nc.tensor.matmul(query_ps[:], wq_blocks[:, b, :], query_nodes, start=True, stop=True)
             key_ps = psum.tile([P, EDGES], F32, name="key_ps")
-            nc.tensor.matmul(key_ps[:], wk_sb[:, rows], key_nodes, start=True, stop=True)
+            nc.tensor.matmul(key_ps[:], wk_blocks[:, b, :], key_nodes, start=True, stop=True)
 
             query_sb = work.tile([P, EDGES], F32, name="query_sb")
-            nc.scalar.activation(query_sb[:], query_ps[:], IDENTITY, bias=biases[:, h : h + 1])
+            nc.scalar.activation(query_sb[:], query_ps[:], IDENTITY, bias=bq_sb[:, b : b + 1])
             product = work.tile([P, EDGES], F32, name="product")
             nc.vector.scalar_tensor_tensor(
-                product[:], key_ps[:], biases[:, HEADS + h : HEADS + h + 1], query_sb[:], ADD, MULT
+                product[:], key_ps[:], bk_sb[:, b : b + 1], query_sb[:], ADD, MULT
             )
-            nc.sync.dma_start(out[rows, :], product[:])
+            nc.sync.dma_start(out_blocks[b], product[:])

@@ -41,19 +41,37 @@ def tile_attentionheads_kernel(tc, x, wq, bq, wk, bk, offs, out):
         out_blocks = out.rearrange("(r b) e -> b r e", b=BLOCKS)
 
         half = EDGES // PER_COLUMN
-        query_nodes = nodes[:].indirect(offsets[:, 0:half])
-        key_nodes = nodes[:].indirect(offsets[:, half : 2 * half])
 
-        for b in range(BLOCKS):
+        def project_query(b):
             query_ps = psum.tile([P, EDGES], F32, name="query_ps")
-            nc.tensor.matmul(query_ps[:], wq_blocks[:, b, :], query_nodes, start=True, stop=True)
-            key_ps = psum.tile([P, EDGES], F32, name="key_ps")
-            nc.tensor.matmul(key_ps[:], wk_blocks[:, b, :], key_nodes, start=True, stop=True)
-
+            nc.tensor.matmul(
+                query_ps[:], wq_blocks[:, b, :], nodes[:].indirect(offsets[:, 0:half]),
+                start=True, stop=True,
+            )
             query_sb = work.tile([P, EDGES], F32, name="query_sb")
             nc.scalar.activation(query_sb[:], query_ps[:], IDENTITY, bias=bq_sb[:, b : b + 1])
-            product = work.tile([P, EDGES], F32, name="product")
-            nc.vector.scalar_tensor_tensor(
-                product[:], key_ps[:], bk_sb[:, b : b + 1], query_sb[:], ADD, MULT
-            )
-            nc.sync.dma_start(out_blocks[b], product[:])
+            return query_sb
+
+        def finish_block(b, query_sb, pieces):
+            width = EDGES // pieces
+            for piece in range(pieces):
+                edges = slice(piece * width, (piece + 1) * width)
+                first = half + piece * width // PER_COLUMN
+                key_ps = psum.tile([P, width], F32, name="key_ps")
+                nc.tensor.matmul(
+                    key_ps[:], wk_blocks[:, b, :],
+                    nodes[:].indirect(offsets[:, first : first + width // PER_COLUMN]),
+                    start=True, stop=True,
+                )
+                product = work.tile([P, width], F32, name="product")
+                nc.vector.scalar_tensor_tensor(
+                    product[:], key_ps[:], bk_sb[:, b : b + 1], query_sb[:, edges], ADD, MULT
+                )
+                nc.sync.dma_start(out_blocks[b][:, edges], product[:])
+
+        query_sb = project_query(0)
+        for b in range(BLOCKS):
+            last = b == BLOCKS - 1
+            next_query_sb = None if last else project_query(b + 1)
+            finish_block(b, query_sb, pieces=2 if last else 1)
+            query_sb = next_query_sb

@@ -18,27 +18,29 @@ def tile_attentionheads_kernel(tc, x, wq, bq, wk, bk, offs, out):
     nc = tc.nc
     with (
         tc.tile_pool(name="held", bufs=1) as held,
-        tc.tile_pool(name="work", bufs=BLOCKS) as work,
+        tc.tile_pool(name="work", bufs=BLOCKS + 1) as work,
         tc.psum_pool(name="psum", bufs=BLOCKS) as psum,
     ):
+        out_blocks = out.rearrange("(r b) e -> b r e", b=BLOCKS)
+
         offsets = held.tile([P, LIST // PER_COLUMN], U16, name="offsets")
         nc.sync.dma_start(offsets[:], offs)
-        nodes = held.tile([P, NODES], BF16, name="nodes")
-        nc.sync.dma_start(nodes[:], x)
         wq_sb = held.tile([P, BLOCKS * P], BF16, name="wq_sb")
         nc.scalar.dma_start(wq_sb[:], wq)
         wk_sb = held.tile([P, BLOCKS * P], BF16, name="wk_sb")
-        nc.scalar.dma_start(wk_sb[:], wk)
-
+        nc.sync.dma_start(wk_sb[:], wk)
         bq_sb = held.tile([P, BLOCKS], F32, name="bq_sb")
         nc.scalar.dma_start(bq_sb[:], bq.rearrange("(r b) o -> r (b o)", b=BLOCKS))
         bk_sb = held.tile([P, BLOCKS], F32, name="bk_sb")
         nc.scalar.dma_start(bk_sb[:], bk.rearrange("(r b) o -> r (b o)", b=BLOCKS))
+        nodes = held.tile([P, NODES], BF16, name="nodes")
+        nc.sync.dma_start(nodes[:, 0 : NODES // 2], x[:, 0 : NODES // 2])
+        nc.scalar.dma_start(nodes[:, NODES // 2 : NODES], x[:, NODES // 2 : NODES])
+
         wq_blocks = held.tile([P, BLOCKS, P], BF16, name="wq_blocks")
         nc.vector.tensor_copy(wq_blocks[:], wq_sb[:].rearrange("f (r b) -> f b r", b=BLOCKS))
         wk_blocks = held.tile([P, BLOCKS, P], BF16, name="wk_blocks")
-        nc.scalar.activation(wk_blocks[:], wk_sb[:].rearrange("f (r b) -> f b r", b=BLOCKS), IDENTITY)
-        out_blocks = out.rearrange("(r b) e -> b r e", b=BLOCKS)
+        nc.vector.tensor_copy(wk_blocks[:], wk_sb[:].rearrange("f (r b) -> f b r", b=BLOCKS))
 
         half = EDGES // PER_COLUMN
 

@@ -11,6 +11,8 @@ EDGES = 512
 LIST = 2 * EDGES
 PER_COLUMN = 16
 
+WARM_MATMULS = 5
+
 FLOPS = 2 * P * (BLOCKS * P) * LIST
 
 
@@ -19,7 +21,9 @@ def tile_attentionheads_kernel(tc, x, wq, bq, wk, bk, offs, out):
     with (
         tc.tile_pool(name="held", bufs=1) as held,
         tc.tile_pool(name="work", bufs=BLOCKS + 1) as work,
-        tc.psum_pool(name="psum", bufs=BLOCKS) as psum,
+        tc.psum_pool(name="query_banks", bufs=BLOCKS) as query_banks,
+        tc.psum_pool(name="key_banks", bufs=BLOCKS - 1) as key_banks,
+        tc.psum_pool(name="spare_bank", bufs=1) as spare_bank,
     ):
         out_blocks = out.rearrange("(r b) e -> b r e", b=BLOCKS)
 
@@ -42,10 +46,16 @@ def tile_attentionheads_kernel(tc, x, wq, bq, wk, bk, offs, out):
         wk_blocks = held.tile([P, BLOCKS, P], BF16, name="wk_blocks")
         nc.vector.tensor_copy(wk_blocks[:], wk_sb[:].rearrange("f (r b) -> f b r", b=BLOCKS))
 
+        zeros = held.tile([P, EDGES], BF16, name="zeros")
+        nc.vector.memset(zeros[:], 0.0)
+        unread = spare_bank.tile([P, EDGES], F32, name="unread")
+        for i in range(WARM_MATMULS):
+            nc.tensor.matmul(unread[:], zeros[:, 0:P], zeros[:], start=True, stop=True)
+
         half = EDGES // PER_COLUMN
 
         def project_query(b):
-            query_ps = psum.tile([P, EDGES], F32, name="query_ps")
+            query_ps = query_banks.tile([P, EDGES], F32, name="query_ps")
             nc.tensor.matmul(
                 query_ps[:], wq_blocks[:, b, :], nodes[:].indirect(offsets[:, 0:half]),
                 start=True, stop=True,
@@ -59,7 +69,7 @@ def tile_attentionheads_kernel(tc, x, wq, bq, wk, bk, offs, out):
             for piece in range(pieces):
                 edges = slice(piece * width, (piece + 1) * width)
                 first = half + piece * width // PER_COLUMN
-                key_ps = psum.tile([P, width], F32, name="key_ps")
+                key_ps = key_banks.tile([P, width], F32, name="key_ps")
                 nc.tensor.matmul(
                     key_ps[:], wk_blocks[:, b, :],
                     nodes[:].indirect(offsets[:, first : first + width // PER_COLUMN]),

@@ -11,8 +11,6 @@ EDGES = 512
 LIST = 2 * EDGES
 PER_COLUMN = 16
 
-WARM_MATMULS = 5
-
 FLOPS = 2 * P * (BLOCKS * P) * LIST
 
 
@@ -21,9 +19,7 @@ def tile_attentionheads_kernel(tc, x, wq, bq, wk, bk, offs, out):
     with (
         tc.tile_pool(name="held", bufs=1) as held,
         tc.tile_pool(name="work", bufs=BLOCKS + 1) as work,
-        tc.psum_pool(name="query_banks", bufs=BLOCKS) as query_banks,
-        tc.psum_pool(name="key_banks", bufs=BLOCKS - 1) as key_banks,
-        tc.psum_pool(name="spare_bank", bufs=1) as spare_bank,
+        tc.psum_pool(name="psum", bufs=BLOCKS) as psum,
     ):
         out_blocks = out.rearrange("(r b) e -> b r e", b=BLOCKS)
 
@@ -33,29 +29,27 @@ def tile_attentionheads_kernel(tc, x, wq, bq, wk, bk, offs, out):
         nc.scalar.dma_start(wq_sb[:], wq)
         wk_sb = held.tile([P, BLOCKS * P], BF16, name="wk_sb")
         nc.sync.dma_start(wk_sb[:], wk)
-        bq_sb = held.tile([P, BLOCKS], F32, name="bq_sb")
-        nc.scalar.dma_start(bq_sb[:], bq.rearrange("(r b) o -> r (b o)", b=BLOCKS))
-        bk_sb = held.tile([P, BLOCKS], F32, name="bk_sb")
-        nc.scalar.dma_start(bk_sb[:], bk.rearrange("(r b) o -> r (b o)", b=BLOCKS))
         nodes = held.tile([P, NODES], BF16, name="nodes")
         nc.sync.dma_start(nodes[:, 0 : NODES // 2], x[:, 0 : NODES // 2])
         nc.scalar.dma_start(nodes[:, NODES // 2 : NODES], x[:, NODES // 2 : NODES])
+        bq_sb = held.tile([P, BLOCKS], F32, name="bq_sb")
+        nc.scalar.dma_start(bq_sb[:], bq.rearrange("(r b) o -> r (b o)", b=BLOCKS))
+        bk_sb = held.tile([P, BLOCKS], F32, name="bk_sb")
+        nc.sync.dma_start(bk_sb[:], bk.rearrange("(r b) o -> r (b o)", b=BLOCKS))
+
+        scratch = held.tile([P, 2], F32, name="scratch")
+        nc.vector.memset(scratch[:, 0:1], 0.0)
+        nc.scalar.activation(scratch[:, 1:2], scratch[:, 0:1], IDENTITY)
 
         wq_blocks = held.tile([P, BLOCKS, P], BF16, name="wq_blocks")
         nc.vector.tensor_copy(wq_blocks[:], wq_sb[:].rearrange("f (r b) -> f b r", b=BLOCKS))
         wk_blocks = held.tile([P, BLOCKS, P], BF16, name="wk_blocks")
         nc.vector.tensor_copy(wk_blocks[:], wk_sb[:].rearrange("f (r b) -> f b r", b=BLOCKS))
 
-        zeros = held.tile([P, EDGES], BF16, name="zeros")
-        nc.vector.memset(zeros[:], 0.0)
-        unread = spare_bank.tile([P, EDGES], F32, name="unread")
-        for i in range(WARM_MATMULS):
-            nc.tensor.matmul(unread[:], zeros[:, 0:P], zeros[:], start=True, stop=True)
-
         half = EDGES // PER_COLUMN
 
         def project_query(b):
-            query_ps = query_banks.tile([P, EDGES], F32, name="query_ps")
+            query_ps = psum.tile([P, EDGES], F32, name="query_ps")
             nc.tensor.matmul(
                 query_ps[:], wq_blocks[:, b, :], nodes[:].indirect(offsets[:, 0:half]),
                 start=True, stop=True,
@@ -69,7 +63,7 @@ def tile_attentionheads_kernel(tc, x, wq, bq, wk, bk, offs, out):
             for piece in range(pieces):
                 edges = slice(piece * width, (piece + 1) * width)
                 first = half + piece * width // PER_COLUMN
-                key_ps = key_banks.tile([P, width], F32, name="key_ps")
+                key_ps = psum.tile([P, width], F32, name="key_ps")
                 nc.tensor.matmul(
                     key_ps[:], wk_blocks[:, b, :],
                     nodes[:].indirect(offsets[:, first : first + width // PER_COLUMN]),

@@ -46,38 +46,40 @@ def tile_attentionheads_kernel(tc, x, wq, bq, wk, bk, offs, out):
         wk_blocks = held.tile([P, BLOCKS, P], BF16, name="wk_blocks")
         nc.vector.tensor_copy(wk_blocks[:], wk_sb[:].rearrange("f (r b) -> f b r", b=BLOCKS))
 
-        half = EDGES // PER_COLUMN
-
-        def project_query(b):
-            query_ps = psum.tile([P, EDGES], F32, name="query_ps")
+        def gathered_product(weight_blocks, b, entry, width, name):
+            product_ps = psum.tile([P, width], F32, name=name)
+            first = entry // PER_COLUMN
             nc.tensor.matmul(
-                query_ps[:], wq_blocks[:, b, :], nodes[:].indirect(offsets[:, 0:half]),
+                product_ps[:], weight_blocks[:, b, :],
+                nodes[:].indirect(offsets[:, first : first + width // PER_COLUMN]),
                 start=True, stop=True,
             )
-            query_sb = work.tile([P, EDGES], F32, name="query_sb")
-            nc.scalar.activation(query_sb[:], query_ps[:], IDENTITY, bias=bq_sb[:, b : b + 1])
-            return query_sb
+            return product_ps
 
-        def finish_block(b, query_sb, pieces):
+        def project_query(b, pieces):
             width = EDGES // pieces
+            query_pieces = []
             for piece in range(pieces):
-                edges = slice(piece * width, (piece + 1) * width)
-                first = half + piece * width // PER_COLUMN
-                key_ps = psum.tile([P, width], F32, name="key_ps")
-                nc.tensor.matmul(
-                    key_ps[:], wk_blocks[:, b, :],
-                    nodes[:].indirect(offsets[:, first : first + width // PER_COLUMN]),
-                    start=True, stop=True,
-                )
+                query_ps = gathered_product(wq_blocks, b, piece * width, width, "query_ps")
+                query_sb = work.tile([P, width], F32, name="query_sb")
+                nc.scalar.activation(query_sb[:], query_ps[:], IDENTITY, bias=bq_sb[:, b : b + 1])
+                query_pieces.append(query_sb)
+            return query_pieces
+
+        def finish_block(b, query_pieces):
+            width = EDGES // len(query_pieces)
+            for piece, query_sb in enumerate(query_pieces):
+                key_ps = gathered_product(wk_blocks, b, EDGES + piece * width, width, "key_ps")
                 product = work.tile([P, width], F32, name="product")
                 nc.vector.scalar_tensor_tensor(
-                    product[:], key_ps[:], bk_sb[:, b : b + 1], query_sb[:, edges], ADD, MULT
+                    product[:], key_ps[:], bk_sb[:, b : b + 1], query_sb[:], ADD, MULT
                 )
-                nc.sync.dma_start(out_blocks[b][:, edges], product[:])
+                nc.sync.dma_start(out_blocks[b][:, piece * width : (piece + 1) * width], product[:])
 
-        query_sb = project_query(0)
-        for b in range(BLOCKS):
-            last = b == BLOCKS - 1
-            next_query_sb = None if last else project_query(b + 1)
-            finish_block(b, query_sb, pieces=2 if last else 1)
-            query_sb = next_query_sb
+        ahead = project_query(0, pieces=1)
+        for b in range(BLOCKS - 1):
+            query_pieces = ahead
+            if b + 1 < BLOCKS - 1:
+                ahead = project_query(b + 1, pieces=1)
+            finish_block(b, query_pieces)
+        finish_block(BLOCKS - 1, project_query(BLOCKS - 1, pieces=2))

@@ -30,8 +30,10 @@ def tile_attentionheads_kernel(tc, x, wq, bq, wk, bk, offs, out):
         wk_sb = held.tile([P, BLOCKS * P], BF16, name="wk_sb")
         nc.sync.dma_start(wk_sb[:], wk)
         nodes = held.tile([P, NODES], BF16, name="nodes")
-        nc.sync.dma_start(nodes[:, 0 : NODES // 2], x[:, 0 : NODES // 2])
-        nc.scalar.dma_start(nodes[:, NODES // 2 : NODES], x[:, NODES // 2 : NODES])
+        quarter = NODES // 4
+        for piece, queue in enumerate((nc.sync, nc.scalar, nc.sync, nc.scalar)):
+            columns = slice(piece * quarter, (piece + 1) * quarter)
+            queue.dma_start(nodes[:, columns], x[:, columns])
         bq_sb = held.tile([P, BLOCKS], F32, name="bq_sb")
         nc.scalar.dma_start(bq_sb[:], bq.rearrange("(r b) o -> r (b o)", b=BLOCKS))
         bk_sb = held.tile([P, BLOCKS], F32, name="bk_sb")

@@ -28,7 +28,7 @@ def tile_attentionheads_kernel(tc, x, wq, bq, wk, bk, offs, out):
         wq_sb = held.tile([P, BLOCKS * P], BF16, name="wq_sb")
         nc.scalar.dma_start(wq_sb[:], wq)
         wk_sb = held.tile([P, BLOCKS * P], BF16, name="wk_sb")
-        nc.sync.dma_start(wk_sb[:], wk)
+        nc.gpsimd.dma_start(wk_sb[:], wk)
         nodes = held.tile([P, NODES], BF16, name="nodes")
         quarter = NODES // 4
         for piece, queue in enumerate((nc.sync, nc.scalar, nc.sync, nc.scalar)):

@@ -43,16 +43,23 @@ def tile_attentionheads_kernel(tc, x, wq, bq, wk, bk, offs, out):
         nc.vector.memset(scratch[:, 0:1], 0.0)
         nc.scalar.activation(scratch[:, 1:2], scratch[:, 0:1], IDENTITY)
 
-        wq_blocks = held.tile([P, BLOCKS, P], BF16, name="wq_blocks")
-        nc.vector.tensor_copy(wq_blocks[:], wq_sb[:].rearrange("f (r b) -> f b r", b=BLOCKS))
-        wk_blocks = held.tile([P, BLOCKS, P], BF16, name="wk_blocks")
-        nc.vector.tensor_copy(wk_blocks[:], wk_sb[:].rearrange("f (r b) -> f b r", b=BLOCKS))
+        def regrouped(weights_sb, name):
+            columns_of_block = weights_sb[:].rearrange("f (r b) -> f b r", b=BLOCKS)
+            blocks = []
+            for b in range(BLOCKS):
+                block = held.tile([P, P], BF16, name="%s%d" % (name, b))
+                nc.vector.tensor_copy(block[:], columns_of_block[:, b, :])
+                blocks.append(block)
+            return blocks
+
+        wq_blocks = regrouped(wq_sb, "wq_block")
+        wk_blocks = regrouped(wk_sb, "wk_block")
 
         def gathered_product(weight_blocks, b, entry, width, name):
             product_ps = psum.tile([P, width], F32, name=name)
             first = entry // PER_COLUMN
             nc.tensor.matmul(
-                product_ps[:], weight_blocks[:, b, :],
+                product_ps[:], weight_blocks[b][:],
                 nodes[:].indirect(offsets[:, first : first + width // PER_COLUMN]),
                 start=True, stop=True,
             )

@@ -43,23 +43,14 @@ def tile_attentionheads_kernel(tc, x, wq, bq, wk, bk, offs, out):
         nc.vector.memset(scratch[:, 0:1], 0.0)
         nc.scalar.activation(scratch[:, 1:2], scratch[:, 0:1], IDENTITY)
 
-        def regrouped(weights_sb, name):
-            columns_of_block = weights_sb[:].rearrange("f (r b) -> f b r", b=BLOCKS)
-            blocks = []
-            for b in range(BLOCKS):
-                block = held.tile([P, P], BF16, name="%s%d" % (name, b))
-                nc.vector.tensor_copy(block[:], columns_of_block[:, b, :])
-                blocks.append(block)
-            return blocks
-
-        wq_blocks = regrouped(wq_sb, "wq_block")
-        wk_blocks = regrouped(wk_sb, "wk_block")
+        wq_blocks = wq_sb[:].rearrange("f (r b) -> f b r", b=BLOCKS)
+        wk_blocks = wk_sb[:].rearrange("f (r b) -> f b r", b=BLOCKS)
 
         def gathered_product(weight_blocks, b, entry, width, name):
             product_ps = psum.tile([P, width], F32, name=name)
             first = entry // PER_COLUMN
             nc.tensor.matmul(
-                product_ps[:], weight_blocks[b][:],
+                product_ps[:], weight_blocks[:, b, :],
                 nodes[:].indirect(offsets[:, first : first + width // PER_COLUMN]),
                 start=True, stop=True,
             )

@@ -26,22 +26,23 @@ def tile_attentionheads_kernel(tc, x, wq, bq, wk, bk, offs, out):
         offsets = held.tile([P, LIST // PER_COLUMN], U16, name="offsets")
         nc.sync.dma_start(offsets[:], offs)
         wq_sb = held.tile([P, BLOCKS * P], BF16, name="wq_sb")
-        nc.scalar.dma_start(wq_sb[:], wq)
-        wk_sb = held.tile([P, BLOCKS * P], BF16, name="wk_sb")
-        nc.gpsimd.dma_start(wk_sb[:], wk)
+        nc.sync.dma_start(wq_sb[:], wq)
         nodes = held.tile([P, NODES], BF16, name="nodes")
         quarter = NODES // 4
-        for piece, queue in enumerate((nc.sync, nc.scalar, nc.sync, nc.scalar)):
+        for piece in range(4):
             columns = slice(piece * quarter, (piece + 1) * quarter)
-            queue.dma_start(nodes[:, columns], x[:, columns])
+            nc.sync.dma_start(nodes[:, columns], x[:, columns])
+
         bq_sb = held.tile([P, BLOCKS], F32, name="bq_sb")
         nc.scalar.dma_start(bq_sb[:], bq.rearrange("(r b) o -> r (b o)", b=BLOCKS))
         bk_sb = held.tile([P, BLOCKS], F32, name="bk_sb")
-        nc.sync.dma_start(bk_sb[:], bk.rearrange("(r b) o -> r (b o)", b=BLOCKS))
+        nc.scalar.dma_start(bk_sb[:], bk.rearrange("(r b) o -> r (b o)", b=BLOCKS))
 
-        scratch = held.tile([P, 2], F32, name="scratch")
-        nc.vector.memset(scratch[:, 0:1], 0.0)
-        nc.scalar.activation(scratch[:, 1:2], scratch[:, 0:1], IDENTITY)
+        wk_sb = held.tile([P, BLOCKS * P], BF16, name="wk_sb")
+        zero = held.tile([P, 1], F32, name="zero")
+        nc.vector.memset(zero[:], 0.0)
+        nc.scalar.activation(wk_sb[:, 0:1], zero[:], IDENTITY)
+        nc.scalar.dma_start(wk_sb[:], wk)
 
         wq_blocks = wq_sb[:].rearrange("f (r b) -> f b r", b=BLOCKS)
         wk_blocks = wk_sb[:].rearrange("f (r b) -> f b r", b=BLOCKS)

@@ -34,9 +34,9 @@ def tile_attentionheads_kernel(tc, x, wq, bq, wk, bk, offs, out):
             nc.sync.dma_start(nodes[:, columns], x[:, columns])
 
         bq_sb = held.tile([P, BLOCKS], F32, name="bq_sb")
-        nc.scalar.dma_start(bq_sb[:], bq.rearrange("(r b) o -> r (b o)", b=BLOCKS))
+        nc.sync.dma_start(bq_sb[:], bq.rearrange("(r b) o -> r (b o)", b=BLOCKS))
         bk_sb = held.tile([P, BLOCKS], F32, name="bk_sb")
-        nc.scalar.dma_start(bk_sb[:], bk.rearrange("(r b) o -> r (b o)", b=BLOCKS))
+        nc.sync.dma_start(bk_sb[:], bk.rearrange("(r b) o -> r (b o)", b=BLOCKS))
 
         wk_sb = held.tile([P, BLOCKS * P], BF16, name="wk_sb")
         zero = held.tile([P, 1], F32, name="zero")

@@ -21,12 +21,13 @@ def tile_attentionheads_kernel(tc, x, wq, bq, wk, bk, offs, out):
         tc.tile_pool(name="work", bufs=BLOCKS + 1) as work,
         tc.psum_pool(name="psum", bufs=BLOCKS) as psum,
     ):
-        out_blocks = out.rearrange("(r b) e -> b r e", b=BLOCKS)
+        out_blocks = out.rearrange("(c r s) e -> c s r e", c=2, s=2)
 
+        half = BLOCKS * P // 2
         offsets = held.tile([P, LIST // PER_COLUMN], U16, name="offsets")
         nc.sync.dma_start(offsets[:], offs)
-        wq_sb = held.tile([P, BLOCKS * P], BF16, name="wq_sb")
-        nc.sync.dma_start(wq_sb[:], wq)
+        wq_first = held.tile([P, half], BF16, name="wq_first")
+        nc.sync.dma_start(wq_first[:], wq[:, :half])
         nodes = held.tile([P, NODES], BF16, name="nodes")
         quarter = NODES // 4
         for piece in range(4):
@@ -34,24 +35,32 @@ def tile_attentionheads_kernel(tc, x, wq, bq, wk, bk, offs, out):
             nc.sync.dma_start(nodes[:, columns], x[:, columns])
 
         bq_sb = held.tile([P, BLOCKS], F32, name="bq_sb")
-        nc.sync.dma_start(bq_sb[:], bq.rearrange("(r b) o -> r (b o)", b=BLOCKS))
+        nc.sync.dma_start(
+            bq_sb[:].rearrange("r (c s) -> r c s", s=2), bq.rearrange("(c r s) o -> r c (s o)", c=2, s=2)
+        )
         bk_sb = held.tile([P, BLOCKS], F32, name="bk_sb")
-        nc.sync.dma_start(bk_sb[:], bk.rearrange("(r b) o -> r (b o)", b=BLOCKS))
+        nc.sync.dma_start(
+            bk_sb[:].rearrange("r (c s) -> r c s", s=2), bk.rearrange("(c r s) o -> r c (s o)", c=2, s=2)
+        )
 
-        wk_sb = held.tile([P, BLOCKS * P], BF16, name="wk_sb")
-        zero = held.tile([P, 1], F32, name="zero")
-        nc.vector.memset(zero[:], 0.0)
-        nc.scalar.activation(wk_sb[:, 0:1], zero[:], IDENTITY)
-        nc.scalar.dma_start(wk_sb[:], wk)
+        late_weights = held.tile([P, 3 * half], BF16, name="late_weights")
+        seam = 2 * half
+        zeros = held.tile([P, 2], F32, name="zeros")
+        nc.vector.memset(zeros[:], 0.0)
+        nc.scalar.activation(late_weights[:, seam - 1 : seam + 1], zeros[:], IDENTITY)
+        nc.scalar.dma_start(late_weights[:, :seam], wk)
+        nc.scalar.dma_start(late_weights[:, seam:], wq[:, half:])
 
-        wq_blocks = wq_sb[:].rearrange("f (r b) -> f b r", b=BLOCKS)
-        wk_blocks = wk_sb[:].rearrange("f (r b) -> f b r", b=BLOCKS)
+        wq_halves = (wq_first[:], late_weights[:, seam:])
+        wk_halves = (late_weights[:, :half], late_weights[:, half:seam])
 
-        def gathered_product(weight_blocks, b, entry, width, name):
+        def gathered_product(weight_halves, b, entry, width, name):
             product_ps = psum.tile([P, width], F32, name=name)
             first = entry // PER_COLUMN
+            c, s = divmod(b, 2)
+            weights = weight_halves[c].rearrange("f (r s) -> f s r", s=2)
             nc.tensor.matmul(
-                product_ps[:], weight_blocks[:, b, :],
+                product_ps[:], weights[:, s, :],
                 nodes[:].indirect(offsets[:, first : first + width // PER_COLUMN]),
                 start=True, stop=True,
             )
@@ -61,7 +70,7 @@ def tile_attentionheads_kernel(tc, x, wq, bq, wk, bk, offs, out):
             width = EDGES // pieces
             query_pieces = []
             for piece in range(pieces):
-                query_ps = gathered_product(wq_blocks, b, piece * width, width, "query_ps")
+                query_ps = gathered_product(wq_halves, b, piece * width, width, "query_ps")
                 query_sb = work.tile([P, width], F32, name="query_sb")
                 nc.scalar.activation(query_sb[:], query_ps[:], IDENTITY, bias=bq_sb[:, b : b + 1])
                 query_pieces.append(query_sb)
@@ -70,12 +79,13 @@ def tile_attentionheads_kernel(tc, x, wq, bq, wk, bk, offs, out):
         def finish_block(b, query_pieces):
             width = EDGES // len(query_pieces)
             for piece, query_sb in enumerate(query_pieces):
-                key_ps = gathered_product(wk_blocks, b, EDGES + piece * width, width, "key_ps")
+                key_ps = gathered_product(wk_halves, b, EDGES + piece * width, width, "key_ps")
                 product = work.tile([P, width], F32, name="product")
                 nc.vector.scalar_tensor_tensor(
                     product[:], key_ps[:], bk_sb[:, b : b + 1], query_sb[:], ADD, MULT
                 )
-                nc.sync.dma_start(out_blocks[b][:, piece * width : (piece + 1) * width], product[:])
+                c, s = divmod(b, 2)
+                nc.sync.dma_start(out_blocks[c, s][:, piece * width : (piece + 1) * width], product[:])
 
         ahead = project_query(0, pieces=1)
         for b in range(BLOCKS - 1):

@@ -44,15 +44,16 @@ def tile_attentionheads_kernel(tc, x, wq, bq, wk, bk, offs, out):
         )
 
         late_weights = held.tile([P, 3 * half], BF16, name="late_weights")
-        seam = 2 * half
-        zeros = held.tile([P, 2], F32, name="zeros")
+        late_halves = late_weights[:].rearrange("f (h m) -> f h m", h=3)
+        zeros = held.tile([P, 3], F32, name="zeros")
         nc.vector.memset(zeros[:], 0.0)
-        nc.scalar.activation(late_weights[:, seam - 1 : seam + 1], zeros[:], IDENTITY)
-        nc.scalar.dma_start(late_weights[:, :seam], wk)
-        nc.scalar.dma_start(late_weights[:, seam:], wq[:, half:])
+        nc.scalar.activation(late_halves[:, :, 0], zeros[:], IDENTITY)
+        nc.scalar.dma_start(late_halves[:, 0, :], wk[:, :half])
+        nc.scalar.dma_start(late_halves[:, 1, :], wq[:, half:])
+        nc.scalar.dma_start(late_halves[:, 2, :], wk[:, half:])
 
-        wq_halves = (wq_first[:], late_weights[:, seam:])
-        wk_halves = (late_weights[:, :half], late_weights[:, half:seam])
+        wq_halves = (wq_first[:], late_halves[:, 1, :])
+        wk_halves = (late_halves[:, 0, :], late_halves[:, 2, :])
 
         def gathered_product(weight_halves, b, entry, width, name):
             product_ps = psum.tile([P, width], F32, name=name)

@@ -24,13 +24,14 @@ def tile_attentionheads_kernel(tc, x, wq, bq, wk, bk, offs, out):
         out_blocks = out.rearrange("(c r s) e -> c s r e", c=2, s=2)
 
         half = BLOCKS * P // 2
+        quarter = NODES // 4
+        nodes = held.tile([P, NODES], BF16, name="nodes")
+        nc.sync.dma_start(nodes[:, :quarter], x[:, :quarter])
         offsets = held.tile([P, LIST // PER_COLUMN], U16, name="offsets")
         nc.sync.dma_start(offsets[:], offs)
         wq_first = held.tile([P, half], BF16, name="wq_first")
         nc.sync.dma_start(wq_first[:], wq[:, :half])
-        nodes = held.tile([P, NODES], BF16, name="nodes")
-        quarter = NODES // 4
-        for piece in range(4):
+        for piece in range(1, 4):
             columns = slice(piece * quarter, (piece + 1) * quarter)
             nc.sync.dma_start(nodes[:, columns], x[:, columns])
 

import concourse.mybir as mybir

BF16, F32, U16 = mybir.dt.bfloat16, mybir.dt.float32, mybir.dt.uint16
ADD, MULT = mybir.AluOpType.add, mybir.AluOpType.mult
IDENTITY = mybir.ActivationFunctionType.Identity

P = 128
NODES = 2048
BLOCKS = 4
EDGES = 512
LIST = 2 * EDGES
PER_COLUMN = 16

FLOPS = 2 * P * (BLOCKS * P) * LIST


def tile_attentionheads_kernel(tc, x, wq, bq, wk, bk, offs, out):
    nc = tc.nc
    with (
        tc.tile_pool(name="held", bufs=1) as held,
        tc.tile_pool(name="work", bufs=BLOCKS + 1) as work,
        tc.psum_pool(name="psum", bufs=BLOCKS) as psum,
    ):
        out_blocks = out.rearrange("(c r s) e -> c s r e", c=2, s=2)

        half = BLOCKS * P // 2
        quarter = NODES // 4
        nodes = held.tile([P, NODES], BF16, name="nodes")
        nc.sync.dma_start(nodes[:, :quarter], x[:, :quarter])
        offsets = held.tile([P, LIST // PER_COLUMN], U16, name="offsets")
        nc.sync.dma_start(offsets[:], offs)
        wq_first = held.tile([P, half], BF16, name="wq_first")
        nc.sync.dma_start(wq_first[:], wq[:, :half])
        for piece in range(1, 4):
            columns = slice(piece * quarter, (piece + 1) * quarter)
            nc.sync.dma_start(nodes[:, columns], x[:, columns])

        bq_sb = held.tile([P, BLOCKS], F32, name="bq_sb")
        nc.sync.dma_start(
            bq_sb[:].rearrange("r (c s) -> r c s", s=2), bq.rearrange("(c r s) o -> r c (s o)", c=2, s=2)
        )
        bk_sb = held.tile([P, BLOCKS], F32, name="bk_sb")
        nc.sync.dma_start(
            bk_sb[:].rearrange("r (c s) -> r c s", s=2), bk.rearrange("(c r s) o -> r c (s o)", c=2, s=2)
        )

        late_weights = held.tile([P, 3 * half], BF16, name="late_weights")
        late_halves = late_weights[:].rearrange("f (h m) -> f h m", h=3)
        zeros = held.tile([P, 3], F32, name="zeros")
        nc.vector.memset(zeros[:], 0.0)
        nc.scalar.activation(late_halves[:, :, 0], zeros[:], IDENTITY)
        nc.scalar.dma_start(late_halves[:, 0, :], wk[:, :half])
        nc.scalar.dma_start(late_halves[:, 1, :], wq[:, half:])
        nc.scalar.dma_start(late_halves[:, 2, :], wk[:, half:])

        wq_halves = (wq_first[:], late_halves[:, 1, :])
        wk_halves = (late_halves[:, 0, :], late_halves[:, 2, :])

        def gathered_product(weight_halves, b, entry, width, name):
            product_ps = psum.tile([P, width], F32, name=name)
            first = entry // PER_COLUMN
            c, s = divmod(b, 2)
            weights = weight_halves[c].rearrange("f (r s) -> f s r", s=2)
            nc.tensor.matmul(
                product_ps[:], weights[:, s, :],
                nodes[:].indirect(offsets[:, first : first + width // PER_COLUMN]),
                start=True, stop=True,
            )
            return product_ps

        def project_query(b, pieces):
            width = EDGES // pieces
            query_pieces = []
            for piece in range(pieces):
                query_ps = gathered_product(wq_halves, b, piece * width, width, "query_ps")
                query_sb = work.tile([P, width], F32, name="query_sb")
                nc.scalar.activation(query_sb[:], query_ps[:], IDENTITY, bias=bq_sb[:, b : b + 1])
                query_pieces.append(query_sb)
            return query_pieces

        def finish_block(b, query_pieces):
            width = EDGES // len(query_pieces)
            for piece, query_sb in enumerate(query_pieces):
                key_ps = gathered_product(wk_halves, b, EDGES + piece * width, width, "key_ps")
                product = work.tile([P, width], F32, name="product")
                nc.vector.scalar_tensor_tensor(
                    product[:], key_ps[:], bk_sb[:, b : b + 1], query_sb[:], ADD, MULT
                )
                c, s = divmod(b, 2)
                nc.sync.dma_start(out_blocks[c, s][:, piece * width : (piece + 1) * width], product[:])

        ahead = project_query(0, pieces=1)
        for b in range(BLOCKS - 1):
            query_pieces = ahead
            if b + 1 < BLOCKS - 1:
                ahead = project_query(b + 1, pieces=1)
            finish_block(b, query_pieces)
        finish_block(BLOCKS - 1, project_query(BLOCKS - 1, pieces=2))
